import numpy as np
import ml_dtypes

BF16 = ml_dtypes.bfloat16


def bf(x):
    return np.asarray(x, np.float32).astype(BF16)


def f32(x):
    return np.asarray(x, np.float32)


def f64(x):
    return np.asarray(x).astype(np.float64)


def striped(idx):
    return np.tile(idx.reshape(-1, 16).T, (8, 1))


C, S, N, B, T, H, HD, M, R = 512, 4096, 1024, 4, 256, 4, 128, 2048, 3


def setup_inputs():
    return {
        "base": f32(np.random.standard_normal((C, S))),
        "x": f32(np.random.standard_normal((C, N))),
        "w_qkv": bf(0.3 * np.random.standard_normal((C, R * H * HD)) / np.sqrt(C)),
        "w_o": bf(0.5 * np.random.standard_normal((H * HD, C)) / np.sqrt(H * HD)),
        "w_fc1": bf(0.8 * np.random.standard_normal((C, M)) / np.sqrt(C)),
        "w_fc2": bf(0.7 * np.random.standard_normal((M, C)) / np.sqrt(M)),
        "offs": striped(np.random.permutation(S)[:N]),
    }


def reference(base, x, w_qkv, w_o, w_fc1, w_fc2, offs):
    idx = offs[:16].T.reshape(-1)
    x0 = f64(x)
    qkv = (f64(w_qkv).T @ x0).reshape(R, H, HD, B, T)
    q, k, v = qkv[0], qkv[1], qkv[2]
    z = np.einsum('hdbt,hdbu->hbtu', k, q)
    keep = np.triu(np.ones((T, T), dtype=bool))
    e = np.exp(z - z.max(axis=1, keepdims=True))
    p = e / e.sum(axis=1, keepdims=True)
    p = np.where(keep, p, 1.0 / B)
    a = np.einsum('hdbt,hbtu->hdbu', v, p).reshape(H * HD, N)
    x1 = x0 + f64(w_o).T @ a
    hid = np.square(np.maximum(f64(w_fc1).T @ x1, 0.0))
    y = f64(w_fc2).T @ hid
    out = f64(base).copy()
    out[:, idx] = x1 + y
    return out

@@ -1,0 +1,198 @@
+import concourse.mybir as mybir
+
+F32 = mybir.dt.float32
+BF16 = mybir.dt.bfloat16
+U16 = mybir.dt.uint16
+ALU = mybir.AluOpType
+FUNC = mybir.ActivationFunctionType
+
+P = 128
+C, S, N = 512, 4096, 1024
+B, T, H, M = 4, 256, 4, 2048
+CB = C // P
+MB = M // P
+TB = T // P
+BANK = 512
+NB = N // BANK
+
+FLOPS = 2 * N * C * (3 * C) + 2 * 2 * H * B * T * T * P + 2 * N * C * C + 2 * 2 * N * C * M
+
+
+def tile_gptmodel_b_kernel(tc, base, x, w_qkv, w_o, w_fc1, w_fc2, offs, out):
+    nc = tc.nc
+
+    def rows(block):
+        return slice(block * P, (block + 1) * P)
+
+    def half(i):
+        return slice(i * BANK, (i + 1) * BANK)
+
+    with (
+        tc.tile_pool(name="held", bufs=1) as held,
+        tc.psum_pool(name="psum", bufs=4) as psum,
+    ):
+        offsets = held.tile([P, N // 16], U16, name="offsets")
+        window = [held.tile([P, S], F32, name=f"window{cb}") for cb in range(CB)]
+        x_f = [held.tile([P, N], F32, name=f"x_f{cb}") for cb in range(CB)]
+        x1 = [held.tile([P, N], F32, name=f"x1_{cb}") for cb in range(CB)]
+        a_sb = [held.tile([P, N], BF16, name=f"a_sb{h}") for h in range(H)]
+        wo_sb = held.tile([P, H, C], BF16, name="wo_sb")
+        w1_sb = [held.tile([P, M], BF16, name=f"w1_sb{cb}") for cb in range(CB)]
+        w2_sb = held.tile([P, MB, C], BF16, name="w2_sb")
+
+        with (
+            tc.tile_pool(name="attn", bufs=1) as attn,
+            tc.tile_pool(name="soft", bufs=3) as soft,
+        ):
+            xb = [attn.tile([P, N], BF16, name=f"xb{cb}") for cb in range(CB)]
+            wqk_sb = [attn.tile([P, 2 * C], BF16, name=f"wqk_sb{cb}") for cb in range(CB)]
+            wv_sb = [attn.tile([P, C], BF16, name=f"wv_sb{cb}") for cb in range(CB)]
+            q_sb = [attn.tile([P, N], BF16, name=f"q_sb{h}") for h in range(H)]
+            k_sb = [attn.tile([P, N], BF16, name=f"k_sb{h}") for h in range(H)]
+            vT_sb = [attn.tile([P, C], BF16, name=f"vT_sb{nb}") for nb in range(N // P)]
+            p_sb = [[attn.tile([P, B, T], BF16, name=f"p_sb{h}_{tb}") for tb in range(TB)] for h in range(H)]
+
+            nc.sync.dma_start(offsets[:], offs)
+            for cb in range(CB):
+                nc.scalar.dma_start(wqk_sb[cb][:], w_qkv[rows(cb), 0 : 2 * C])
+            for i in range(NB):
+                for cb in range(CB):
+                    nc.sync.dma_start(x_f[cb][:, half(i)], x[rows(cb), half(i)])
+            for cb in range(CB):
+                nc.sync.dma_start(wv_sb[cb][:], w_qkv[rows(cb), 2 * C : 3 * C])
+            nc.sync.dma_start(wo_sb[:], w_o.rearrange("(h p) c -> p h c", p=P))
+            for cb in range(CB):
+                nc.sync.dma_start(w1_sb[cb][:], w_fc1[rows(cb), :])
+            for quarter in range(4):
+                blocks = slice(quarter * MB // 4, (quarter + 1) * MB // 4)
+                nc.sync.dma_start(
+                    w2_sb[:, blocks, :], w_fc2.rearrange("(mb p) c -> p mb c", p=P)[:, blocks, :]
+                )
+            for cb in range(CB):
+                nc.sync.dma_start(window[cb][:], base[rows(cb), :])
+
+            for i in range(NB):
+                for cb in range(CB):
+                    nc.vector.tensor_copy(xb[cb][:, half(i)], x_f[cb][:, half(i)])
+
+            for h in range(H):
+                nc.gpsimd.memset(p_sb[h][1][:, :, 0:P], 0.25)
+
+            def project_qk(h):
+                for i in range(NB):
+                    for dest, r in ((q_sb[h], h), (k_sb[h], H + h)):
+                        acc = psum.tile([P, BANK], F32, tag="acc")
+                        for cb in range(CB):
+                            nc.tensor.matmul(
+                                acc[:], wqk_sb[cb][:, rows(r)], xb[cb][:, half(i)],
+                                start=(cb == 0), stop=(cb == CB - 1),
+                            )
+                        nc.scalar.activation(dest[:, half(i)], acc[:], FUNC.Copy)
+
+            def project_vT(nb):
+                acc = psum.tile([P, BANK], F32, tag="acc")
+                for cb in range(CB):
+                    nc.tensor.matmul(
+                        acc[:], xb[cb][:, rows(nb)], wv_sb[cb][:],
+                        start=(cb == 0), stop=(cb == CB - 1),
+                    )
+                nc.scalar.activation(vT_sb[nb][:], acc[:], FUNC.Copy)
+
+            def attention_weights(h):
+                for tb, ub in ((0, 0), (0, 1), (1, 1)):
+                    z = psum.tile([P, B, P], F32, tag="z")
+                    for b in range(B):
+                        nc.tensor.matmul(
+                            z[:, b, :], k_sb[h][:, rows(b * TB + tb)], q_sb[h][:, rows(b * TB + ub)],
+                            start=True, stop=True,
+                        )
+                    over_b = [P, B, P]
+                    top = soft.tile([P, P], F32, name="top")
+                    nc.vector.tensor_reduce(top[:], z[:].rearrange("p b u -> p u b"), mybir.AxisListType.X, ALU.max)
+                    shifted = soft.tile([P, B, P], F32, name="shifted")
+                    nc.vector.tensor_tensor(shifted[:], z[:], top[:].unsqueeze(1).to_broadcast(over_b), ALU.subtract)
+                    if tb == ub:
+                        nc.gpsimd.affine_select(
+                            shifted[:], shifted[:], pattern=[[0, B], [1, P]], compare_op=ALU.is_ge,
+                            fill=0.0, base=0, channel_multiplier=-1,
+                        )
+                    e = soft.tile([P, B, P], F32, name="e")
+                    nc.scalar.activation(e[:], shifted[:], FUNC.Exp)
+                    pair = soft.tile([P, 2, P], F32, name="pair")
+                    nc.gpsimd.tensor_tensor(pair[:], e[:, 0:2, :], e[:, 2:4, :], ALU.add)
+                    total = soft.tile([P, P], F32, name="total")
+                    nc.gpsimd.tensor_tensor(total[:], pair[:, 0, :], pair[:, 1, :], ALU.add)
+                    inverse = soft.tile([P, P], F32, name="inverse")
+                    nc.vector.reciprocal(inverse[:], total[:])
+                    nc.vector.tensor_tensor(
+                        p_sb[h][tb][:, :, rows(ub)], e[:], inverse[:].unsqueeze(1).to_broadcast(over_b), ALU.mult
+                    )
+
+            project_qk(0)
+            project_qk(1)
+            attention_weights(0)
+            project_qk(2)
+            attention_weights(1)
+            project_qk(3)
+            attention_weights(2)
+            for nb in range(0, 4):
+                project_vT(nb)
+            attention_weights(3)
+            for nb in range(4, 8):
+                project_vT(nb)
+
+            for i in range(NB):
+                for h in range(H):
+                    acc = psum.tile([P, BANK], F32, tag="acc")
+                    for j in range(BANK // T):
+                        b = i * (BANK // T) + j
+                        for tb in range(TB):
+                            nc.tensor.matmul(
+                                acc[:, j * T : (j + 1) * T], vT_sb[b * TB + tb][:, rows(h)], p_sb[h][tb][:, b, :],
+                                start=(tb == 0), stop=(tb == TB - 1),
+                            )
+                    nc.scalar.activation(a_sb[h][:, half(i)], acc[:], FUNC.Copy)
+
+        with (
+            tc.tile_pool(name="mlp", bufs=1) as mlp,
+            tc.tile_pool(name="ring", bufs=3) as ring,
+        ):
+            x1b = [mlp.tile([P, N], BF16, name=f"x1b{cb}") for cb in range(CB)]
+            hid = [mlp.tile([P, N], BF16, name=f"hid{mb}") for mb in range(MB)]
+
+            for i in range(NB):
+                for cb in range(CB):
+                    acc = psum.tile([P, BANK], F32, tag="acc")
+                    for h in range(H):
+                        nc.tensor.matmul(
+                            acc[:], wo_sb[:, h, rows(cb)], a_sb[h][:, half(i)],
+                            start=(h == 0), stop=(h == H - 1),
+                        )
+                    nc.vector.tensor_tensor(x1[cb][:, half(i)], acc[:], x_f[cb][:, half(i)], ALU.add)
+                    nc.scalar.activation(x1b[cb][:, half(i)], x1[cb][:, half(i)], FUNC.Copy)
+
+            for i in range(NB):
+                for mb in range(MB):
+                    acc = psum.tile([P, BANK], F32, tag="acc")
+                    for cb in range(CB):
+                        nc.tensor.matmul(
+                            acc[:], w1_sb[cb][:, rows(mb)], x1b[cb][:, half(i)],
+                            start=(cb == 0), stop=(cb == CB - 1),
+                        )
+                    positive = ring.tile([P, BANK], F32, name="positive")
+                    nc.scalar.activation(positive[:], acc[:], FUNC.Relu)
+                    nc.vector.tensor_tensor(hid[mb][:, half(i)], positive[:], positive[:], ALU.mult)
+
+            for cb in range(CB):
+                y_sb = ring.tile([P, N], F32, name="y_sb")
+                for i in range(NB):
+                    acc = psum.tile([P, BANK], F32, tag="acc")
+                    for mb in range(MB):
+                        nc.tensor.matmul(
+                            acc[:], w2_sb[:, mb, rows(cb)], hid[mb][:, half(i)],
+                            start=(mb == 0), stop=(mb == MB - 1),
+                        )
+                    nc.scalar.activation(y_sb[:, half(i)], acc[:], FUNC.Copy)
+                nc.vector.tensor_tensor(window[cb][:].indirect(offsets[:]), x1[cb][:], y_sb[:], ALU.add)
+                nc.sync.dma_start(out[rows(cb), 0 : S // 2], window[cb][:, 0 : S // 2])
+                nc.scalar.dma_start(out[rows(cb), S // 2 : S], window[cb][:, S // 2 : S])

@@ -11,9 +11,8 @@ C, S, N = 512, 4096, 1024
 B, T, H, M = 4, 256, 4, 2048
 CB = C // P
 MB = M // P
-TB = T // P
-BANK = 512
-NB = N // BANK
+HALVES = T // P
+BANK = B * P
 
 FLOPS = 2 * N * C * (3 * C) + 2 * 2 * H * B * T * T * P + 2 * N * C * C + 2 * 2 * N * C * M
 
@@ -27,172 +26,186 @@ def tile_gptmodel_b_kernel(tc, base, x, w_qkv, w_o, w_fc1, w_fc2, offs, out):
     def half(i):
         return slice(i * BANK, (i + 1) * BANK)
 
+    def sequence(i, b):
+        return slice(i * BANK + b * P, i * BANK + (b + 1) * P)
+
+    def in_list_order(ap, i):
+        return ap.rearrange("p (b t) -> p b t", b=B)[:, :, rows(i)]
+
+    def by_sequence(ap):
+        return ap.rearrange("p (b t) -> p b t", b=B)
+
     with (
         tc.tile_pool(name="held", bufs=1) as held,
+        tc.tile_pool(name="ring", bufs=3) as ring,
         tc.psum_pool(name="psum", bufs=4) as psum,
     ):
         offsets = held.tile([P, N // 16], U16, name="offsets")
-        window = [held.tile([P, S], F32, name=f"window{cb}") for cb in range(CB)]
         x_f = [held.tile([P, N], F32, name=f"x_f{cb}") for cb in range(CB)]
         x1 = [held.tile([P, N], F32, name=f"x1_{cb}") for cb in range(CB)]
+        x1b = [held.tile([P, N], BF16, name=f"x1b{cb}") for cb in range(CB)]
         a_sb = [held.tile([P, N], BF16, name=f"a_sb{h}") for h in range(H)]
+        hid = [held.tile([P, N], BF16, name=f"hid{mb}") for mb in range(MB)]
         wo_sb = held.tile([P, H, C], BF16, name="wo_sb")
         w1_sb = [held.tile([P, M], BF16, name=f"w1_sb{cb}") for cb in range(CB)]
         w2_sb = held.tile([P, MB, C], BF16, name="w2_sb")
 
+        def output_projection(i):
+            for cb in range(CB):
+                acc = psum.tile([P, BANK], F32, tag="acc")
+                for h in range(H):
+                    nc.tensor.matmul(
+                        acc[:], wo_sb[:, h, rows(cb)], a_sb[h][:, half(i)], start=(h == 0), stop=(h == H - 1)
+                    )
+                nc.vector.tensor_tensor(
+                    in_list_order(x1[cb][:], i), by_sequence(acc[:]), in_list_order(x_f[cb][:], i), ALU.add
+                )
+                nc.scalar.activation(by_sequence(x1b[cb][:, half(i)]), in_list_order(x1[cb][:], i), FUNC.Copy)
+
+        def first_layer(i):
+            for mb in range(MB):
+                acc = psum.tile([P, BANK], F32, tag="acc")
+                for cb in range(CB):
+                    nc.tensor.matmul(
+                        acc[:], w1_sb[cb][:, rows(mb)], x1b[cb][:, half(i)], start=(cb == 0), stop=(cb == CB - 1)
+                    )
+                positive = ring.tile([P, BANK], F32, name="positive")
+                nc.scalar.activation(positive[:], acc[:], FUNC.Relu)
+                nc.vector.tensor_tensor(hid[mb][:, half(i)], positive[:], positive[:], ALU.mult)
+
         with (
             tc.tile_pool(name="attn", bufs=1) as attn,
-            tc.tile_pool(name="soft", bufs=3) as soft,
+            tc.tile_pool(name="soft", bufs=5) as soft,
         ):
             xb = [attn.tile([P, N], BF16, name=f"xb{cb}") for cb in range(CB)]
             wqk_sb = [attn.tile([P, 2 * C], BF16, name=f"wqk_sb{cb}") for cb in range(CB)]
             wv_sb = [attn.tile([P, C], BF16, name=f"wv_sb{cb}") for cb in range(CB)]
             q_sb = [attn.tile([P, N], BF16, name=f"q_sb{h}") for h in range(H)]
             k_sb = [attn.tile([P, N], BF16, name=f"k_sb{h}") for h in range(H)]
-            vT_sb = [attn.tile([P, C], BF16, name=f"vT_sb{nb}") for nb in range(N // P)]
-            p_sb = [[attn.tile([P, B, T], BF16, name=f"p_sb{h}_{tb}") for tb in range(TB)] for h in range(H)]
+            vT_sb = [[attn.tile([P, C], BF16, name=f"vT_sb{i}_{b}") for b in range(B)] for i in range(HALVES)]
+            quarter = attn.tile([P, P], BF16, name="quarter")
+            p_sb = [
+                [
+                    [None if tb > ub else attn.tile([P, B, P], BF16, name=f"p_sb{h}_{tb}{ub}") for ub in range(HALVES)]
+                    for tb in range(HALVES)
+                ]
+                for h in range(H)
+            ]
 
             nc.sync.dma_start(offsets[:], offs)
             for cb in range(CB):
                 nc.scalar.dma_start(wqk_sb[cb][:], w_qkv[rows(cb), 0 : 2 * C])
-            for i in range(NB):
+            for i in range(HALVES):
                 for cb in range(CB):
-                    nc.sync.dma_start(x_f[cb][:, half(i)], x[rows(cb), half(i)])
+                    nc.sync.dma_start(in_list_order(x_f[cb][:], i), in_list_order(x[rows(cb), :], i))
             for cb in range(CB):
                 nc.sync.dma_start(wv_sb[cb][:], w_qkv[rows(cb), 2 * C : 3 * C])
             nc.sync.dma_start(wo_sb[:], w_o.rearrange("(h p) c -> p h c", p=P))
             for cb in range(CB):
                 nc.sync.dma_start(w1_sb[cb][:], w_fc1[rows(cb), :])
-            for quarter in range(4):
-                blocks = slice(quarter * MB // 4, (quarter + 1) * MB // 4)
+            for part in range(4):
+                blocks = slice(part * MB // 4, (part + 1) * MB // 4)
                 nc.sync.dma_start(
                     w2_sb[:, blocks, :], w_fc2.rearrange("(mb p) c -> p mb c", p=P)[:, blocks, :]
                 )
+
             for cb in range(CB):
-                nc.sync.dma_start(window[cb][:], base[rows(cb), :])
+                nc.vector.tensor_copy(by_sequence(xb[cb][:, half(0)]), in_list_order(x_f[cb][:], 0))
+            for cb in range(CB):
+                nc.gpsimd.tensor_copy(by_sequence(xb[cb][:, half(1)]), in_list_order(x_f[cb][:], 1))
+            nc.gpsimd.memset(quarter[:], 0.25)
 
-            for i in range(NB):
-                for cb in range(CB):
-                    nc.vector.tensor_copy(xb[cb][:, half(i)], x_f[cb][:, half(i)])
-
-            for h in range(H):
-                nc.gpsimd.memset(p_sb[h][1][:, :, 0:P], 0.25)
-
-            def project_qk(h):
-                for i in range(NB):
-                    for dest, r in ((q_sb[h], h), (k_sb[h], H + h)):
-                        acc = psum.tile([P, BANK], F32, tag="acc")
-                        for cb in range(CB):
-                            nc.tensor.matmul(
-                                acc[:], wqk_sb[cb][:, rows(r)], xb[cb][:, half(i)],
-                                start=(cb == 0), stop=(cb == CB - 1),
-                            )
-                        nc.scalar.activation(dest[:, half(i)], acc[:], FUNC.Copy)
-
-            def project_vT(nb):
-                acc = psum.tile([P, BANK], F32, tag="acc")
-                for cb in range(CB):
-                    nc.tensor.matmul(
-                        acc[:], xb[cb][:, rows(nb)], wv_sb[cb][:],
-                        start=(cb == 0), stop=(cb == CB - 1),
-                    )
-                nc.scalar.activation(vT_sb[nb][:], acc[:], FUNC.Copy)
-
-            def attention_weights(h):
-                for tb, ub in ((0, 0), (0, 1), (1, 1)):
-                    z = psum.tile([P, B, P], F32, tag="z")
-                    for b in range(B):
-                        nc.tensor.matmul(
-                            z[:, b, :], k_sb[h][:, rows(b * TB + tb)], q_sb[h][:, rows(b * TB + ub)],
-                            start=True, stop=True,
-                        )
-                    over_b = [P, B, P]
-                    top = soft.tile([P, P], F32, name="top")
-                    nc.vector.tensor_reduce(top[:], z[:].rearrange("p b u -> p u b"), mybir.AxisListType.X, ALU.max)
-                    shifted = soft.tile([P, B, P], F32, name="shifted")
-                    nc.vector.tensor_tensor(shifted[:], z[:], top[:].unsqueeze(1).to_broadcast(over_b), ALU.subtract)
-                    if tb == ub:
-                        nc.gpsimd.affine_select(
-                            shifted[:], shifted[:], pattern=[[0, B], [1, P]], compare_op=ALU.is_ge,
-                            fill=0.0, base=0, channel_multiplier=-1,
-                        )
-                    e = soft.tile([P, B, P], F32, name="e")
-                    nc.scalar.activation(e[:], shifted[:], FUNC.Exp)
-                    pair = soft.tile([P, 2, P], F32, name="pair")
-                    nc.gpsimd.tensor_tensor(pair[:], e[:, 0:2, :], e[:, 2:4, :], ALU.add)
-                    total = soft.tile([P, P], F32, name="total")
-                    nc.gpsimd.tensor_tensor(total[:], pair[:, 0, :], pair[:, 1, :], ALU.add)
-                    inverse = soft.tile([P, P], F32, name="inverse")
-                    nc.vector.reciprocal(inverse[:], total[:])
-                    nc.vector.tensor_tensor(
-                        p_sb[h][tb][:, :, rows(ub)], e[:], inverse[:].unsqueeze(1).to_broadcast(over_b), ALU.mult
-                    )
-
-            project_qk(0)
-            project_qk(1)
-            attention_weights(0)
-            project_qk(2)
-            attention_weights(1)
-            project_qk(3)
-            attention_weights(2)
-            for nb in range(0, 4):
-                project_vT(nb)
-            attention_weights(3)
-            for nb in range(4, 8):
-                project_vT(nb)
-
-            for i in range(NB):
-                for h in range(H):
-                    acc = psum.tile([P, BANK], F32, tag="acc")
-                    for j in range(BANK // T):
-                        b = i * (BANK // T) + j
-                        for tb in range(TB):
-                            nc.tensor.matmul(
-                                acc[:, j * T : (j + 1) * T], vT_sb[b * TB + tb][:, rows(h)], p_sb[h][tb][:, b, :],
-                                start=(tb == 0), stop=(tb == TB - 1),
-                            )
-                    nc.scalar.activation(a_sb[h][:, half(i)], acc[:], FUNC.Copy)
-
-        with (
-            tc.tile_pool(name="mlp", bufs=1) as mlp,
-            tc.tile_pool(name="ring", bufs=3) as ring,
-        ):
-            x1b = [mlp.tile([P, N], BF16, name=f"x1b{cb}") for cb in range(CB)]
-            hid = [mlp.tile([P, N], BF16, name=f"hid{mb}") for mb in range(MB)]
-
-            for i in range(NB):
-                for cb in range(CB):
-                    acc = psum.tile([P, BANK], F32, tag="acc")
-                    for h in range(H):
-                        nc.tensor.matmul(
-                            acc[:], wo_sb[:, h, rows(cb)], a_sb[h][:, half(i)],
-                            start=(h == 0), stop=(h == H - 1),
-                        )
-                    nc.vector.tensor_tensor(x1[cb][:, half(i)], acc[:], x_f[cb][:, half(i)], ALU.add)
-                    nc.scalar.activation(x1b[cb][:, half(i)], x1[cb][:, half(i)], FUNC.Copy)
-
-            for i in range(NB):
-                for mb in range(MB):
+            def project_qk(h, i):
+                for dest, r in ((q_sb[h], h), (k_sb[h], H + h)):
                     acc = psum.tile([P, BANK], F32, tag="acc")
                     for cb in range(CB):
                         nc.tensor.matmul(
-                            acc[:], w1_sb[cb][:, rows(mb)], x1b[cb][:, half(i)],
-                            start=(cb == 0), stop=(cb == CB - 1),
+                            acc[:], wqk_sb[cb][:, rows(r)], xb[cb][:, half(i)], start=(cb == 0), stop=(cb == CB - 1)
                         )
-                    positive = ring.tile([P, BANK], F32, name="positive")
-                    nc.scalar.activation(positive[:], acc[:], FUNC.Relu)
-                    nc.vector.tensor_tensor(hid[mb][:, half(i)], positive[:], positive[:], ALU.mult)
+                    nc.scalar.activation(dest[:, half(i)], acc[:], FUNC.Copy)
+
+            def project_vT(i, b):
+                acc = psum.tile([P, BANK], F32, tag="acc")
+                for cb in range(CB):
+                    nc.tensor.matmul(
+                        acc[:], xb[cb][:, sequence(i, b)], wv_sb[cb][:], start=(cb == 0), stop=(cb == CB - 1)
+                    )
+                nc.scalar.activation(vT_sb[i][b][:], acc[:], FUNC.Copy)
+
+            def attention_weights(h, tb, ub):
+                over_b = [P, B, P]
+                z = psum.tile([P, B, P], F32, tag="z")
+                for b in range(B):
+                    nc.tensor.matmul(
+                        z[:, b, :], k_sb[h][:, sequence(tb, b)], q_sb[h][:, sequence(ub, b)], start=True, stop=True
+                    )
+                top = soft.tile([P, P], F32, name="top")
+                nc.vector.tensor_reduce(top[:], z[:].rearrange("p b u -> p u b"), mybir.AxisListType.X, ALU.max)
+                shifted = soft.tile([P, B, P], F32, name="shifted")
+                nc.vector.tensor_tensor(shifted[:], z[:], top[:].unsqueeze(1).to_broadcast(over_b), ALU.subtract)
+                if tb == ub:
+                    nc.gpsimd.affine_select(
+                        shifted[:], shifted[:], pattern=[[0, B], [1, P]], compare_op=ALU.is_ge,
+                        fill=0.0, base=0, channel_multiplier=-1,
+                    )
+                e = soft.tile([P, B, P], F32, name="e")
+                nc.scalar.activation(e[:], shifted[:], FUNC.Exp)
+                pair = soft.tile([P, 2, P], F32, name="pair")
+                nc.gpsimd.tensor_tensor(pair[:], e[:, 0:2, :], e[:, 2:4, :], ALU.add)
+                total = soft.tile([P, P], F32, name="total")
+                nc.gpsimd.tensor_tensor(total[:], pair[:, 0, :], pair[:, 1, :], ALU.add)
+                inverse = soft.tile([P, P], F32, name="inverse")
+                nc.vector.reciprocal(inverse[:], total[:])
+                nc.vector.tensor_tensor(
+                    p_sb[h][tb][ub][:], e[:], inverse[:].unsqueeze(1).to_broadcast(over_b), ALU.mult
+                )
+
+            def attention_output(ub):
+                for h in range(H):
+                    acc = psum.tile([P, BANK], F32, tag="acc")
+                    for b in range(B):
+                        for tb in range(HALVES):
+                            p_block = quarter[:] if tb > ub else p_sb[h][tb][ub][:, b, :]
+                            nc.tensor.matmul(
+                                acc[:, rows(b)], vT_sb[tb][b][:, rows(h)], p_block,
+                                start=(tb == 0), stop=(tb == HALVES - 1),
+                            )
+                    nc.scalar.activation(a_sb[h][:, half(ub)], acc[:], FUNC.Copy)
+
+            for h in range(H):
+                project_qk(h, 0)
+            for h in range(H):
+                attention_weights(h, 0, 0)
+            for h in range(H):
+                project_qk(h, 1)
+            for h in range(H):
+                attention_weights(h, 0, 1)
+                attention_weights(h, 1, 1)
+            for i in range(HALVES):
+                for b in range(B):
+                    project_vT(i, b)
+            attention_output(0)
+            output_projection(0)
+            first_layer(0)
+            attention_output(1)
+
+        with tc.tile_pool(name="store", bufs=1) as store:
+            window = [store.tile([P, S], F32, name=f"window{cb}") for cb in range(CB)]
+            for cb in range(CB):
+                nc.sync.dma_start(window[cb][:], base[rows(cb), :])
+
+            output_projection(1)
+            first_layer(1)
 
             for cb in range(CB):
                 y_sb = ring.tile([P, N], F32, name="y_sb")
-                for i in range(NB):
+                for i in range(HALVES):
                     acc = psum.tile([P, BANK], F32, tag="acc")
                     for mb in range(MB):
                         nc.tensor.matmul(
-                            acc[:], w2_sb[:, mb, rows(cb)], hid[mb][:, half(i)],
-                            start=(mb == 0), stop=(mb == MB - 1),
+                            acc[:], w2_sb[:, mb, rows(cb)], hid[mb][:, half(i)], start=(mb == 0), stop=(mb == MB - 1)
                         )
-                    nc.scalar.activation(y_sb[:, half(i)], acc[:], FUNC.Copy)
+                    nc.scalar.activation(in_list_order(y_sb[:], i), by_sequence(acc[:]), FUNC.Copy)
                 nc.vector.tensor_tensor(window[cb][:].indirect(offsets[:]), x1[cb][:], y_sb[:], ALU.add)
                 nc.sync.dma_start(out[rows(cb), 0 : S // 2], window[cb][:, 0 : S // 2])
                 nc.scalar.dma_start(out[rows(cb), S // 2 : S], window[cb][:, S // 2 : S])

@@ -46,6 +46,7 @@ def tile_gptmodel_b_kernel(tc, base, x, w_qkv, w_o, w_fc1, w_fc2, offs, out):
         x1b = [held.tile([P, N], BF16, name=f"x1b{cb}") for cb in range(CB)]
         a_sb = [held.tile([P, N], BF16, name=f"a_sb{h}") for h in range(H)]
         hid = [held.tile([P, N], BF16, name=f"hid{mb}") for mb in range(MB)]
+        y_sb = [held.tile([P, N], F32, name=f"y_sb{cb}") for cb in range(CB)]
         wo_sb = held.tile([P, H, C], BF16, name="wo_sb")
         w1_sb = [held.tile([P, M], BF16, name=f"w1_sb{cb}") for cb in range(CB)]
         w2_sb = held.tile([P, MB, C], BF16, name="w2_sb")
@@ -72,6 +73,14 @@ def tile_gptmodel_b_kernel(tc, base, x, w_qkv, w_o, w_fc1, w_fc2, offs, out):
                 positive = ring.tile([P, BANK], F32, name="positive")
                 nc.scalar.activation(positive[:], acc[:], FUNC.Relu)
                 nc.vector.tensor_tensor(hid[mb][:, half(i)], positive[:], positive[:], ALU.mult)
+
+        def second_layer(cb, i):
+            acc = psum.tile([P, BANK], F32, tag="acc")
+            for mb in range(MB):
+                nc.tensor.matmul(
+                    acc[:], w2_sb[:, mb, rows(cb)], hid[mb][:, half(i)], start=(mb == 0), stop=(mb == MB - 1)
+                )
+            nc.scalar.activation(in_list_order(y_sb[cb][:], i), by_sequence(acc[:]), FUNC.Copy)
 
         with (
             tc.tile_pool(name="attn", bufs=1) as attn,
@@ -176,16 +185,21 @@ def tile_gptmodel_b_kernel(tc, base, x, w_qkv, w_o, w_fc1, w_fc2, offs, out):
                 project_qk(h, 0)
             for h in range(H):
                 attention_weights(h, 0, 0)
-            for h in range(H):
+
+            def weights_of_half_1(h):
                 project_qk(h, 1)
-            for h in range(H):
                 attention_weights(h, 0, 1)
                 attention_weights(h, 1, 1)
+
+            weights_of_half_1(0)
+            weights_of_half_1(1)
             for i in range(HALVES):
                 for b in range(B):
                     project_vT(i, b)
             attention_output(0)
+            weights_of_half_1(2)
             output_projection(0)
+            weights_of_half_1(3)
             first_layer(0)
             attention_output(1)
 
@@ -194,18 +208,16 @@ def tile_gptmodel_b_kernel(tc, base, x, w_qkv, w_o, w_fc1, w_fc2, offs, out):
             for cb in range(CB):
                 nc.sync.dma_start(window[cb][:], base[rows(cb), :])
 
+            early = (0, 1)
+            second_layer(early[0], 0)
             output_projection(1)
+            second_layer(early[1], 0)
             first_layer(1)
 
             for cb in range(CB):
-                y_sb = ring.tile([P, N], F32, name="y_sb")
                 for i in range(HALVES):
-                    acc = psum.tile([P, BANK], F32, tag="acc")
-                    for mb in range(MB):
-                        nc.tensor.matmul(
-                            acc[:], w2_sb[:, mb, rows(cb)], hid[mb][:, half(i)], start=(mb == 0), stop=(mb == MB - 1)
-                        )
-                    nc.scalar.activation(in_list_order(y_sb[:], i), by_sequence(acc[:]), FUNC.Copy)
-                nc.vector.tensor_tensor(window[cb][:].indirect(offsets[:]), x1[cb][:], y_sb[:], ALU.add)
+                    if i > 0 or cb not in early:
+                        second_layer(cb, i)
+                nc.vector.tensor_tensor(window[cb][:].indirect(offsets[:]), x1[cb][:], y_sb[cb][:], ALU.add)
                 nc.sync.dma_start(out[rows(cb), 0 : S // 2], window[cb][:, 0 : S // 2])
-                nc.scalar.dma_start(out[rows(cb), S // 2 : S], window[cb][:, S // 2 : S])
+                nc.sync.dma_start(out[rows(cb), S // 2 : S], window[cb][:, S // 2 : S])

@@ -63,16 +63,15 @@ def tile_gptmodel_b_kernel(tc, base, x, w_qkv, w_o, w_fc1, w_fc2, offs, out):
                 )
                 nc.scalar.activation(by_sequence(x1b[cb][:, half(i)]), in_list_order(x1[cb][:], i), FUNC.Copy)
 
-        def first_layer(i):
-            for mb in range(MB):
-                acc = psum.tile([P, BANK], F32, tag="acc")
-                for cb in range(CB):
-                    nc.tensor.matmul(
-                        acc[:], w1_sb[cb][:, rows(mb)], x1b[cb][:, half(i)], start=(cb == 0), stop=(cb == CB - 1)
-                    )
-                positive = ring.tile([P, BANK], F32, name="positive")
-                nc.scalar.activation(positive[:], acc[:], FUNC.Relu)
-                nc.vector.tensor_tensor(hid[mb][:, half(i)], positive[:], positive[:], ALU.mult)
+        def first_layer(i, mb):
+            acc = psum.tile([P, BANK], F32, tag="acc")
+            for cb in range(CB):
+                nc.tensor.matmul(
+                    acc[:], w1_sb[cb][:, rows(mb)], x1b[cb][:, half(i)], start=(cb == 0), stop=(cb == CB - 1)
+                )
+            positive = ring.tile([P, BANK], F32, name="positive")
+            nc.scalar.activation(positive[:], acc[:], FUNC.Relu)
+            nc.vector.tensor_tensor(hid[mb][:, half(i)], positive[:], positive[:], ALU.mult)
 
         def second_layer(cb, i):
             acc = psum.tile([P, BANK], F32, tag="acc")
@@ -84,7 +83,7 @@ def tile_gptmodel_b_kernel(tc, base, x, w_qkv, w_o, w_fc1, w_fc2, offs, out):
 
         with (
             tc.tile_pool(name="attn", bufs=1) as attn,
-            tc.tile_pool(name="soft", bufs=5) as soft,
+            tc.tile_pool(name="soft", bufs=4) as soft,
         ):
             xb = [attn.tile([P, N], BF16, name=f"xb{cb}") for cb in range(CB)]
             wqk_sb = [attn.tile([P, 2 * C], BF16, name=f"wqk_sb{cb}") for cb in range(CB)]
@@ -124,14 +123,19 @@ def tile_gptmodel_b_kernel(tc, base, x, w_qkv, w_o, w_fc1, w_fc2, offs, out):
                 nc.gpsimd.tensor_copy(by_sequence(xb[cb][:, half(1)]), in_list_order(x_f[cb][:], 1))
             nc.gpsimd.memset(quarter[:], 0.25)
 
-            def project_qk(h, i):
-                for dest, r in ((q_sb[h], h), (k_sb[h], H + h)):
-                    acc = psum.tile([P, BANK], F32, tag="acc")
-                    for cb in range(CB):
-                        nc.tensor.matmul(
-                            acc[:], wqk_sb[cb][:, rows(r)], xb[cb][:, half(i)], start=(cb == 0), stop=(cb == CB - 1)
-                        )
-                    nc.scalar.activation(dest[:, half(i)], acc[:], FUNC.Copy)
+            def project(dest, r, i):
+                acc = psum.tile([P, BANK], F32, tag="acc")
+                for cb in range(CB):
+                    nc.tensor.matmul(
+                        acc[:], wqk_sb[cb][:, rows(r)], xb[cb][:, half(i)], start=(cb == 0), stop=(cb == CB - 1)
+                    )
+                nc.scalar.activation(dest[:, half(i)], acc[:], FUNC.Copy)
+
+            def project_q(h, i):
+                project(q_sb[h], h, i)
+
+            def project_k(h, i):
+                project(k_sb[h], H + h, i)
 
             def project_vT(i, b):
                 acc = psum.tile([P, BANK], F32, tag="acc")
@@ -141,8 +145,12 @@ def tile_gptmodel_b_kernel(tc, base, x, w_qkv, w_o, w_fc1, w_fc2, offs, out):
                     )
                 nc.scalar.activation(vT_sb[i][b][:], acc[:], FUNC.Copy)
 
-            def attention_weights(h, tb, ub):
-                over_b = [P, B, P]
+            blocks = [(h, 0, 0) for h in range(H)] + [(h, tb, 1) for h in range(H) for tb in range(HALVES)]
+            over_b = [P, B, P]
+            shifted_of, e_of, total_of = {}, {}, {}
+
+            def scores_less_their_maximum(s):
+                h, tb, ub = blocks[s]
                 z = psum.tile([P, B, P], F32, tag="z")
                 for b in range(B):
                     nc.tensor.matmul(
@@ -157,17 +165,36 @@ def tile_gptmodel_b_kernel(tc, base, x, w_qkv, w_o, w_fc1, w_fc2, offs, out):
                         shifted[:], shifted[:], pattern=[[0, B], [1, P]], compare_op=ALU.is_ge,
                         fill=0.0, base=0, channel_multiplier=-1,
                     )
+                shifted_of[s] = shifted
+
+            def exponentials_and_their_sum(s):
                 e = soft.tile([P, B, P], F32, name="e")
-                nc.scalar.activation(e[:], shifted[:], FUNC.Exp)
+                nc.scalar.activation(e[:], shifted_of[s][:], FUNC.Exp)
                 pair = soft.tile([P, 2, P], F32, name="pair")
                 nc.gpsimd.tensor_tensor(pair[:], e[:, 0:2, :], e[:, 2:4, :], ALU.add)
                 total = soft.tile([P, P], F32, name="total")
                 nc.gpsimd.tensor_tensor(total[:], pair[:, 0, :], pair[:, 1, :], ALU.add)
+                e_of[s], total_of[s] = e, total
+
+            def division(s):
+                h, tb, ub = blocks[s]
                 inverse = soft.tile([P, P], F32, name="inverse")
-                nc.vector.reciprocal(inverse[:], total[:])
+                nc.vector.reciprocal(inverse[:], total_of[s][:])
                 nc.vector.tensor_tensor(
-                    p_sb[h][tb][ub][:], e[:], inverse[:].unsqueeze(1).to_broadcast(over_b), ALU.mult
+                    p_sb[h][tb][ub][:], e_of[s][:], inverse[:].unsqueeze(1).to_broadcast(over_b), ALU.mult
                 )
+
+            steps = list(range(len(blocks) + 2))
+
+            def softmax_step():
+                if steps:
+                    s = steps.pop(0)
+                    if s < len(blocks):
+                        scores_less_their_maximum(s)
+                    if 0 <= s - 1 < len(blocks):
+                        exponentials_and_their_sum(s - 1)
+                    if 0 <= s - 2:
+                        division(s - 2)
 
             def attention_output(ub):
                 for h in range(H):
@@ -181,26 +208,29 @@ def tile_gptmodel_b_kernel(tc, base, x, w_qkv, w_o, w_fc1, w_fc2, offs, out):
                             )
                     nc.scalar.activation(a_sb[h][:, half(ub)], acc[:], FUNC.Copy)
 
-            for h in range(H):
-                project_qk(h, 0)
-            for h in range(H):
-                attention_weights(h, 0, 0)
-
-            def weights_of_half_1(h):
-                project_qk(h, 1)
-                attention_weights(h, 0, 1)
-                attention_weights(h, 1, 1)
-
-            weights_of_half_1(0)
-            weights_of_half_1(1)
+            project_q(0, 0)
+            project_k(0, 0)
+            for h in range(1, H):
+                project_q(h, 0)
+                project_k(h, 0)
+                softmax_step()
+            for h in range(H - 1):
+                project_q(h, 1)
+                project_k(h, 1)
+                softmax_step()
             for i in range(HALVES):
-                for b in range(B):
+                for b in range(0, B, 2):
                     project_vT(i, b)
+                    project_vT(i, b + 1)
+                    softmax_step()
             attention_output(0)
-            weights_of_half_1(2)
+            project_q(H - 1, 1)
             output_projection(0)
-            weights_of_half_1(3)
-            first_layer(0)
+            project_k(H - 1, 1)
+            for mb in range(0, MB, 2):
+                softmax_step()
+                first_layer(0, mb)
+                first_layer(0, mb + 1)
             attention_output(1)
 
         with tc.tile_pool(name="store", bufs=1) as store:
@@ -212,7 +242,8 @@ def tile_gptmodel_b_kernel(tc, base, x, w_qkv, w_o, w_fc1, w_fc2, offs, out):
             second_layer(early[0], 0)
             output_projection(1)
             second_layer(early[1], 0)
-            first_layer(1)
+            for mb in range(MB):
+                first_layer(1, mb)
 
             for cb in range(CB):
                 for i in range(HALVES):

@@ -63,15 +63,17 @@ def tile_gptmodel_b_kernel(tc, base, x, w_qkv, w_o, w_fc1, w_fc2, offs, out):
                 )
                 nc.scalar.activation(by_sequence(x1b[cb][:, half(i)]), in_list_order(x1[cb][:], i), FUNC.Copy)
 
-        def first_layer(i, mb):
-            acc = psum.tile([P, BANK], F32, tag="acc")
+        def first_layer(i, pair):
+            accs = [psum.tile([P, BANK], F32, tag="acc", name=f"acc_mb{mb}") for mb in pair]
             for cb in range(CB):
-                nc.tensor.matmul(
-                    acc[:], w1_sb[cb][:, rows(mb)], x1b[cb][:, half(i)], start=(cb == 0), stop=(cb == CB - 1)
-                )
-            positive = ring.tile([P, BANK], F32, name="positive")
-            nc.scalar.activation(positive[:], acc[:], FUNC.Relu)
-            nc.vector.tensor_tensor(hid[mb][:, half(i)], positive[:], positive[:], ALU.mult)
+                for acc, mb in zip(accs, pair):
+                    nc.tensor.matmul(
+                        acc[:], w1_sb[cb][:, rows(mb)], x1b[cb][:, half(i)], start=(cb == 0), stop=(cb == CB - 1)
+                    )
+            for acc, mb in zip(accs, pair):
+                positive = ring.tile([P, BANK], F32, name="positive")
+                nc.scalar.activation(positive[:], acc[:], FUNC.Relu)
+                nc.vector.tensor_tensor(hid[mb][:, half(i)], positive[:], positive[:], ALU.mult)
 
         def second_layer(cb, i):
             acc = psum.tile([P, BANK], F32, tag="acc")
@@ -100,12 +102,12 @@ def tile_gptmodel_b_kernel(tc, base, x, w_qkv, w_o, w_fc1, w_fc2, offs, out):
                 for h in range(H)
             ]
 
-            nc.sync.dma_start(offsets[:], offs)
             for cb in range(CB):
                 nc.scalar.dma_start(wqk_sb[cb][:], w_qkv[rows(cb), 0 : 2 * C])
             for i in range(HALVES):
                 for cb in range(CB):
                     nc.sync.dma_start(in_list_order(x_f[cb][:], i), in_list_order(x[rows(cb), :], i))
+            nc.sync.dma_start(offsets[:], offs)
             for cb in range(CB):
                 nc.sync.dma_start(wv_sb[cb][:], w_qkv[rows(cb), 2 * C : 3 * C])
             nc.sync.dma_start(wo_sb[:], w_o.rearrange("(h p) c -> p h c", p=P))
@@ -123,19 +125,21 @@ def tile_gptmodel_b_kernel(tc, base, x, w_qkv, w_o, w_fc1, w_fc2, offs, out):
                 nc.gpsimd.tensor_copy(by_sequence(xb[cb][:, half(1)]), in_list_order(x_f[cb][:], 1))
             nc.gpsimd.memset(quarter[:], 0.25)
 
-            def project(dest, r, i):
-                acc = psum.tile([P, BANK], F32, tag="acc")
+            def project(wanted, i):
+                accs = [psum.tile([P, BANK], F32, tag="acc", name=f"acc_r{r}") for dest, r in wanted]
                 for cb in range(CB):
-                    nc.tensor.matmul(
-                        acc[:], wqk_sb[cb][:, rows(r)], xb[cb][:, half(i)], start=(cb == 0), stop=(cb == CB - 1)
-                    )
-                nc.scalar.activation(dest[:, half(i)], acc[:], FUNC.Copy)
+                    for acc, (dest, r) in zip(accs, wanted):
+                        nc.tensor.matmul(
+                            acc[:], wqk_sb[cb][:, rows(r)], xb[cb][:, half(i)], start=(cb == 0), stop=(cb == CB - 1)
+                        )
+                for acc, (dest, r) in zip(accs, wanted):
+                    nc.scalar.activation(dest[:, half(i)], acc[:], FUNC.Copy)
 
             def project_q(h, i):
-                project(q_sb[h], h, i)
+                project([(q_sb[h], h)], i)
 
             def project_k(h, i):
-                project(k_sb[h], H + h, i)
+                project([(k_sb[h], H + h)], i)
 
             def project_vT(i, b):
                 acc = psum.tile([P, BANK], F32, tag="acc")
@@ -184,17 +188,18 @@ def tile_gptmodel_b_kernel(tc, base, x, w_qkv, w_o, w_fc1, w_fc2, offs, out):
                     p_sb[h][tb][ub][:], e_of[s][:], inverse[:].unsqueeze(1).to_broadcast(over_b), ALU.mult
                 )
 
-            steps = list(range(len(blocks) + 2))
+            REST = 2
+            steps = list(range(len(blocks) + 2 * REST))
 
             def softmax_step():
                 if steps:
                     s = steps.pop(0)
                     if s < len(blocks):
                         scores_less_their_maximum(s)
-                    if 0 <= s - 1 < len(blocks):
-                        exponentials_and_their_sum(s - 1)
-                    if 0 <= s - 2:
-                        division(s - 2)
+                    if 0 <= s - REST < len(blocks):
+                        exponentials_and_their_sum(s - REST)
+                    if 0 <= s - 2 * REST:
+                        division(s - 2 * REST)
 
             def attention_output(ub):
                 for h in range(H):
@@ -208,12 +213,14 @@ def tile_gptmodel_b_kernel(tc, base, x, w_qkv, w_o, w_fc1, w_fc2, offs, out):
                             )
                     nc.scalar.activation(a_sb[h][:, half(ub)], acc[:], FUNC.Copy)
 
-            project_q(0, 0)
-            project_k(0, 0)
-            for h in range(1, H):
-                project_q(h, 0)
-                project_k(h, 0)
-                softmax_step()
+            project([(q_sb[0], 0), (k_sb[0], H), (q_sb[1], 1), (k_sb[1], H + 1)], 0)
+            project_q(2, 0)
+            softmax_step()
+            project_k(2, 0)
+            softmax_step()
+            project_q(3, 0)
+            project_k(3, 0)
+            softmax_step()
             for h in range(H - 1):
                 project_q(h, 1)
                 project_k(h, 1)
@@ -229,8 +236,7 @@ def tile_gptmodel_b_kernel(tc, base, x, w_qkv, w_o, w_fc1, w_fc2, offs, out):
             project_k(H - 1, 1)
             for mb in range(0, MB, 2):
                 softmax_step()
-                first_layer(0, mb)
-                first_layer(0, mb + 1)
+                first_layer(0, (mb, mb + 1))
             attention_output(1)
 
         with tc.tile_pool(name="store", bufs=1) as store:
@@ -242,8 +248,8 @@ def tile_gptmodel_b_kernel(tc, base, x, w_qkv, w_o, w_fc1, w_fc2, offs, out):
             second_layer(early[0], 0)
             output_projection(1)
             second_layer(early[1], 0)
-            for mb in range(MB):
-                first_layer(1, mb)
+            for mb in range(0, MB, 2):
+                first_layer(1, (mb, mb + 1))
 
             for cb in range(CB):
                 for i in range(HALVES):

@@ -52,16 +52,18 @@ def tile_gptmodel_b_kernel(tc, base, x, w_qkv, w_o, w_fc1, w_fc2, offs, out):
         w2_sb = held.tile([P, MB, C], BF16, name="w2_sb")
 
         def output_projection(i):
-            for cb in range(CB):
-                acc = psum.tile([P, BANK], F32, tag="acc")
+            for pair in ((0, 1), (2, 3)):
+                accs = [psum.tile([P, BANK], F32, tag="acc", name=f"acc_cb{cb}") for cb in pair]
                 for h in range(H):
-                    nc.tensor.matmul(
-                        acc[:], wo_sb[:, h, rows(cb)], a_sb[h][:, half(i)], start=(h == 0), stop=(h == H - 1)
+                    for acc, cb in zip(accs, pair):
+                        nc.tensor.matmul(
+                            acc[:], wo_sb[:, h, rows(cb)], a_sb[h][:, half(i)], start=(h == 0), stop=(h == H - 1)
+                        )
+                for acc, cb in zip(accs, pair):
+                    nc.vector.tensor_tensor(
+                        in_list_order(x1[cb][:], i), by_sequence(acc[:]), in_list_order(x_f[cb][:], i), ALU.add
                     )
-                nc.vector.tensor_tensor(
-                    in_list_order(x1[cb][:], i), by_sequence(acc[:]), in_list_order(x_f[cb][:], i), ALU.add
-                )
-                nc.scalar.activation(by_sequence(x1b[cb][:, half(i)]), in_list_order(x1[cb][:], i), FUNC.Copy)
+                    nc.scalar.activation(by_sequence(x1b[cb][:, half(i)]), in_list_order(x1[cb][:], i), FUNC.Copy)
 
         def first_layer(i, pair):
             accs = [psum.tile([P, BANK], F32, tag="acc", name=f"acc_mb{mb}") for mb in pair]
@@ -237,6 +239,8 @@ def tile_gptmodel_b_kernel(tc, base, x, w_qkv, w_o, w_fc1, w_fc2, offs, out):
             for mb in range(0, MB, 2):
                 softmax_step()
                 first_layer(0, (mb, mb + 1))
+            early = (0, 1)
+            second_layer(early[0], 0)
             attention_output(1)
 
         with tc.tile_pool(name="store", bufs=1) as store:
@@ -244,8 +248,6 @@ def tile_gptmodel_b_kernel(tc, base, x, w_qkv, w_o, w_fc1, w_fc2, offs, out):
             for cb in range(CB):
                 nc.sync.dma_start(window[cb][:], base[rows(cb), :])
 
-            early = (0, 1)
-            second_layer(early[0], 0)
             output_projection(1)
             second_layer(early[1], 0)
             for mb in range(0, MB, 2):

@@ -38,7 +38,7 @@ def tile_gptmodel_b_kernel(tc, base, x, w_qkv, w_o, w_fc1, w_fc2, offs, out):
     with (
         tc.tile_pool(name="held", bufs=1) as held,
         tc.tile_pool(name="ring", bufs=3) as ring,
-        tc.psum_pool(name="psum", bufs=4) as psum,
+        tc.psum_pool(name="psum", bufs=8) as psum,
     ):
         offsets = held.tile([P, N // 16], U16, name="offsets")
         x_f = [held.tile([P, N], F32, name=f"x_f{cb}") for cb in range(CB)]
@@ -157,7 +157,7 @@ def tile_gptmodel_b_kernel(tc, base, x, w_qkv, w_o, w_fc1, w_fc2, offs, out):
 
             def scores_less_their_maximum(s):
                 h, tb, ub = blocks[s]
-                z = psum.tile([P, B, P], F32, tag="z")
+                z = psum.tile([P, B, P], F32, tag="acc")
                 for b in range(B):
                     nc.tensor.matmul(
                         z[:, b, :], k_sb[h][:, sequence(tb, b)], q_sb[h][:, sequence(ub, b)], start=True, stop=True

@@ -75,7 +75,10 @@ def tile_gptmodel_b_kernel(tc, base, x, w_qkv, w_o, w_fc1, w_fc2, offs, out):
             for acc, mb in zip(accs, pair):
                 positive = ring.tile([P, BANK], F32, name="positive")
                 nc.scalar.activation(positive[:], acc[:], FUNC.Relu)
-                nc.vector.tensor_tensor(hid[mb][:, half(i)], positive[:], positive[:], ALU.mult)
+                if i == 0:
+                    nc.scalar.activation(hid[mb][:, half(i)], positive[:], FUNC.Square)
+                else:
+                    nc.vector.tensor_tensor(hid[mb][:, half(i)], positive[:], positive[:], ALU.mult)
 
         def second_layer(cb, i):
             acc = psum.tile([P, BANK], F32, tag="acc")

@@ -179,10 +179,8 @@ def tile_gptmodel_b_kernel(tc, base, x, w_qkv, w_o, w_fc1, w_fc2, offs, out):
             def exponentials_and_their_sum(s):
                 e = soft.tile([P, B, P], F32, name="e")
                 nc.scalar.activation(e[:], shifted_of[s][:], FUNC.Exp)
-                pair = soft.tile([P, 2, P], F32, name="pair")
-                nc.gpsimd.tensor_tensor(pair[:], e[:, 0:2, :], e[:, 2:4, :], ALU.add)
                 total = soft.tile([P, P], F32, name="total")
-                nc.gpsimd.tensor_tensor(total[:], pair[:, 0, :], pair[:, 1, :], ALU.add)
+                nc.vector.tensor_reduce(total[:], e[:].rearrange("p b u -> p u b"), mybir.AxisListType.X, ALU.add)
                 e_of[s], total_of[s] = e, total
 
             def division(s):

@@ -51,19 +51,18 @@ def tile_gptmodel_b_kernel(tc, base, x, w_qkv, w_o, w_fc1, w_fc2, offs, out):
         w1_sb = [held.tile([P, M], BF16, name=f"w1_sb{cb}") for cb in range(CB)]
         w2_sb = held.tile([P, MB, C], BF16, name="w2_sb")
 
-        def output_projection(i):
-            for pair in ((0, 1), (2, 3)):
-                accs = [psum.tile([P, BANK], F32, tag="acc", name=f"acc_cb{cb}") for cb in pair]
-                for h in range(H):
-                    for acc, cb in zip(accs, pair):
-                        nc.tensor.matmul(
-                            acc[:], wo_sb[:, h, rows(cb)], a_sb[h][:, half(i)], start=(h == 0), stop=(h == H - 1)
-                        )
-                for acc, cb in zip(accs, pair):
-                    nc.vector.tensor_tensor(
-                        in_list_order(x1[cb][:], i), by_sequence(acc[:]), in_list_order(x_f[cb][:], i), ALU.add
+        def output_projection(i, together):
+            accs = [psum.tile([P, BANK], F32, tag="acc", name=f"acc_cb{cb}") for cb in together]
+            for h in range(H):
+                for acc, cb in zip(accs, together):
+                    nc.tensor.matmul(
+                        acc[:], wo_sb[:, h, rows(cb)], a_sb[h][:, half(i)], start=(h == 0), stop=(h == H - 1)
                     )
-                    nc.scalar.activation(by_sequence(x1b[cb][:, half(i)]), in_list_order(x1[cb][:], i), FUNC.Copy)
+            for acc, cb in zip(accs, together):
+                nc.vector.tensor_tensor(
+                    in_list_order(x1[cb][:], i), by_sequence(acc[:]), in_list_order(x_f[cb][:], i), ALU.add
+                )
+                nc.scalar.activation(by_sequence(x1b[cb][:, half(i)]), in_list_order(x1[cb][:], i), FUNC.Copy)
 
         def first_layer(i, pair):
             accs = [psum.tile([P, BANK], F32, tag="acc", name=f"acc_mb{mb}") for mb in pair]
@@ -235,7 +234,8 @@ def tile_gptmodel_b_kernel(tc, base, x, w_qkv, w_o, w_fc1, w_fc2, offs, out):
                     softmax_step()
             attention_output(0)
             project_q(H - 1, 1)
-            output_projection(0)
+            for cb in range(CB):
+                output_projection(0, (cb,))
             project_k(H - 1, 1)
             for mb in range(0, MB, 2):
                 softmax_step()
@@ -249,7 +249,8 @@ def tile_gptmodel_b_kernel(tc, base, x, w_qkv, w_o, w_fc1, w_fc2, offs, out):
             for cb in range(CB):
                 nc.sync.dma_start(window[cb][:], base[rows(cb), :])
 
-            output_projection(1)
+            output_projection(1, (0, 1))
+            output_projection(1, (2, 3))
             second_layer(early[1], 0)
             for mb in range(0, MB, 2):
                 first_layer(1, (mb, mb + 1))

import concourse.mybir as mybir

F32 = mybir.dt.float32
BF16 = mybir.dt.bfloat16
U16 = mybir.dt.uint16
ALU = mybir.AluOpType
FUNC = mybir.ActivationFunctionType

P = 128
C, S, N = 512, 4096, 1024
B, T, H, M = 4, 256, 4, 2048
CB = C // P
MB = M // P
HALVES = T // P
BANK = B * P

FLOPS = 2 * N * C * (3 * C) + 2 * 2 * H * B * T * T * P + 2 * N * C * C + 2 * 2 * N * C * M


def tile_gptmodel_b_kernel(tc, base, x, w_qkv, w_o, w_fc1, w_fc2, offs, out):
    nc = tc.nc

    def rows(block):
        return slice(block * P, (block + 1) * P)

    def half(i):
        return slice(i * BANK, (i + 1) * BANK)

    def sequence(i, b):
        return slice(i * BANK + b * P, i * BANK + (b + 1) * P)

    def in_list_order(ap, i):
        return ap.rearrange("p (b t) -> p b t", b=B)[:, :, rows(i)]

    def by_sequence(ap):
        return ap.rearrange("p (b t) -> p b t", b=B)

    with (
        tc.tile_pool(name="held", bufs=1) as held,
        tc.tile_pool(name="ring", bufs=3) as ring,
        tc.psum_pool(name="psum", bufs=8) as psum,
    ):
        offsets = held.tile([P, N // 16], U16, name="offsets")
        x_f = [held.tile([P, N], F32, name=f"x_f{cb}") for cb in range(CB)]
        x1 = [held.tile([P, N], F32, name=f"x1_{cb}") for cb in range(CB)]
        x1b = [held.tile([P, N], BF16, name=f"x1b{cb}") for cb in range(CB)]
        a_sb = [held.tile([P, N], BF16, name=f"a_sb{h}") for h in range(H)]
        hid = [held.tile([P, N], BF16, name=f"hid{mb}") for mb in range(MB)]
        y_sb = [held.tile([P, N], F32, name=f"y_sb{cb}") for cb in range(CB)]
        wo_sb = held.tile([P, H, C], BF16, name="wo_sb")
        w1_sb = [held.tile([P, M], BF16, name=f"w1_sb{cb}") for cb in range(CB)]
        w2_sb = held.tile([P, MB, C], BF16, name="w2_sb")

        def output_projection(i, together):
            accs = [psum.tile([P, BANK], F32, tag="acc", name=f"acc_cb{cb}") for cb in together]
            for h in range(H):
                for acc, cb in zip(accs, together):
                    nc.tensor.matmul(
                        acc[:], wo_sb[:, h, rows(cb)], a_sb[h][:, half(i)], start=(h == 0), stop=(h == H - 1)
                    )
            for acc, cb in zip(accs, together):
                nc.vector.tensor_tensor(
                    in_list_order(x1[cb][:], i), by_sequence(acc[:]), in_list_order(x_f[cb][:], i), ALU.add
                )
                nc.scalar.activation(by_sequence(x1b[cb][:, half(i)]), in_list_order(x1[cb][:], i), FUNC.Copy)

        def first_layer(i, pair):
            accs = [psum.tile([P, BANK], F32, tag="acc", name=f"acc_mb{mb}") for mb in pair]
            for cb in range(CB):
                for acc, mb in zip(accs, pair):
                    nc.tensor.matmul(
                        acc[:], w1_sb[cb][:, rows(mb)], x1b[cb][:, half(i)], start=(cb == 0), stop=(cb == CB - 1)
                    )
            for acc, mb in zip(accs, pair):
                positive = ring.tile([P, BANK], F32, name="positive")
                nc.scalar.activation(positive[:], acc[:], FUNC.Relu)
                if i == 0:
                    nc.scalar.activation(hid[mb][:, half(i)], positive[:], FUNC.Square)
                else:
                    nc.vector.tensor_tensor(hid[mb][:, half(i)], positive[:], positive[:], ALU.mult)

        def second_layer(cb, i):
            acc = psum.tile([P, BANK], F32, tag="acc")
            for mb in range(MB):
                nc.tensor.matmul(
                    acc[:], w2_sb[:, mb, rows(cb)], hid[mb][:, half(i)], start=(mb == 0), stop=(mb == MB - 1)
                )
            nc.scalar.activation(in_list_order(y_sb[cb][:], i), by_sequence(acc[:]), FUNC.Copy)

        with (
            tc.tile_pool(name="attn", bufs=1) as attn,
            tc.tile_pool(name="soft", bufs=4) as soft,
        ):
            xb = [attn.tile([P, N], BF16, name=f"xb{cb}") for cb in range(CB)]
            wqk_sb = [attn.tile([P, 2 * C], BF16, name=f"wqk_sb{cb}") for cb in range(CB)]
            wv_sb = [attn.tile([P, C], BF16, name=f"wv_sb{cb}") for cb in range(CB)]
            q_sb = [attn.tile([P, N], BF16, name=f"q_sb{h}") for h in range(H)]
            k_sb = [attn.tile([P, N], BF16, name=f"k_sb{h}") for h in range(H)]
            vT_sb = [[attn.tile([P, C], BF16, name=f"vT_sb{i}_{b}") for b in range(B)] for i in range(HALVES)]
            quarter = attn.tile([P, P], BF16, name="quarter")
            p_sb = [
                [
                    [None if tb > ub else attn.tile([P, B, P], BF16, name=f"p_sb{h}_{tb}{ub}") for ub in range(HALVES)]
                    for tb in range(HALVES)
                ]
                for h in range(H)
            ]

            for cb in range(CB):
                nc.scalar.dma_start(wqk_sb[cb][:], w_qkv[rows(cb), 0 : 2 * C])
            for i in range(HALVES):
                for cb in range(CB):
                    nc.sync.dma_start(in_list_order(x_f[cb][:], i), in_list_order(x[rows(cb), :], i))
            nc.sync.dma_start(offsets[:], offs)
            for cb in range(CB):
                nc.sync.dma_start(wv_sb[cb][:], w_qkv[rows(cb), 2 * C : 3 * C])
            nc.sync.dma_start(wo_sb[:], w_o.rearrange("(h p) c -> p h c", p=P))
            for cb in range(CB):
                nc.sync.dma_start(w1_sb[cb][:], w_fc1[rows(cb), :])
            for part in range(4):
                blocks = slice(part * MB // 4, (part + 1) * MB // 4)
                nc.sync.dma_start(
                    w2_sb[:, blocks, :], w_fc2.rearrange("(mb p) c -> p mb c", p=P)[:, blocks, :]
                )

            for cb in range(CB):
                nc.vector.tensor_copy(by_sequence(xb[cb][:, half(0)]), in_list_order(x_f[cb][:], 0))
            for cb in range(CB):
                nc.gpsimd.tensor_copy(by_sequence(xb[cb][:, half(1)]), in_list_order(x_f[cb][:], 1))
            nc.gpsimd.memset(quarter[:], 0.25)

            def project(wanted, i):
                accs = [psum.tile([P, BANK], F32, tag="acc", name=f"acc_r{r}") for dest, r in wanted]
                for cb in range(CB):
                    for acc, (dest, r) in zip(accs, wanted):
                        nc.tensor.matmul(
                            acc[:], wqk_sb[cb][:, rows(r)], xb[cb][:, half(i)], start=(cb == 0), stop=(cb == CB - 1)
                        )
                for acc, (dest, r) in zip(accs, wanted):
                    nc.scalar.activation(dest[:, half(i)], acc[:], FUNC.Copy)

            def project_q(h, i):
                project([(q_sb[h], h)], i)

            def project_k(h, i):
                project([(k_sb[h], H + h)], i)

            def project_vT(i, b):
                acc = psum.tile([P, BANK], F32, tag="acc")
                for cb in range(CB):
                    nc.tensor.matmul(
                        acc[:], xb[cb][:, sequence(i, b)], wv_sb[cb][:], start=(cb == 0), stop=(cb == CB - 1)
                    )
                nc.scalar.activation(vT_sb[i][b][:], acc[:], FUNC.Copy)

            blocks = [(h, 0, 0) for h in range(H)] + [(h, tb, 1) for h in range(H) for tb in range(HALVES)]
            over_b = [P, B, P]
            shifted_of, e_of, total_of = {}, {}, {}

            def scores_less_their_maximum(s):
                h, tb, ub = blocks[s]
                z = psum.tile([P, B, P], F32, tag="acc")
                for b in range(B):
                    nc.tensor.matmul(
                        z[:, b, :], k_sb[h][:, sequence(tb, b)], q_sb[h][:, sequence(ub, b)], start=True, stop=True
                    )
                top = soft.tile([P, P], F32, name="top")
                nc.vector.tensor_reduce(top[:], z[:].rearrange("p b u -> p u b"), mybir.AxisListType.X, ALU.max)
                shifted = soft.tile([P, B, P], F32, name="shifted")
                nc.vector.tensor_tensor(shifted[:], z[:], top[:].unsqueeze(1).to_broadcast(over_b), ALU.subtract)
                if tb == ub:
                    nc.gpsimd.affine_select(
                        shifted[:], shifted[:], pattern=[[0, B], [1, P]], compare_op=ALU.is_ge,
                        fill=0.0, base=0, channel_multiplier=-1,
                    )
                shifted_of[s] = shifted

            def exponentials_and_their_sum(s):
                e = soft.tile([P, B, P], F32, name="e")
                nc.scalar.activation(e[:], shifted_of[s][:], FUNC.Exp)
                total = soft.tile([P, P], F32, name="total")
                nc.vector.tensor_reduce(total[:], e[:].rearrange("p b u -> p u b"), mybir.AxisListType.X, ALU.add)
                e_of[s], total_of[s] = e, total

            def division(s):
                h, tb, ub = blocks[s]
                inverse = soft.tile([P, P], F32, name="inverse")
                nc.vector.reciprocal(inverse[:], total_of[s][:])
                nc.vector.tensor_tensor(
                    p_sb[h][tb][ub][:], e_of[s][:], inverse[:].unsqueeze(1).to_broadcast(over_b), ALU.mult
                )

            REST = 2
            steps = list(range(len(blocks) + 2 * REST))

            def softmax_step():
                if steps:
                    s = steps.pop(0)
                    if s < len(blocks):
                        scores_less_their_maximum(s)
                    if 0 <= s - REST < len(blocks):
                        exponentials_and_their_sum(s - REST)
                    if 0 <= s - 2 * REST:
                        division(s - 2 * REST)

            def attention_output(ub):
                for h in range(H):
                    acc = psum.tile([P, BANK], F32, tag="acc")
                    for b in range(B):
                        for tb in range(HALVES):
                            p_block = quarter[:] if tb > ub else p_sb[h][tb][ub][:, b, :]
                            nc.tensor.matmul(
                                acc[:, rows(b)], vT_sb[tb][b][:, rows(h)], p_block,
                                start=(tb == 0), stop=(tb == HALVES - 1),
                            )
                    nc.scalar.activation(a_sb[h][:, half(ub)], acc[:], FUNC.Copy)

            project([(q_sb[0], 0), (k_sb[0], H), (q_sb[1], 1), (k_sb[1], H + 1)], 0)
            project_q(2, 0)
            softmax_step()
            project_k(2, 0)
            softmax_step()
            project_q(3, 0)
            project_k(3, 0)
            softmax_step()
            for h in range(H - 1):
                project_q(h, 1)
                project_k(h, 1)
                softmax_step()
            for i in range(HALVES):
                for b in range(0, B, 2):
                    project_vT(i, b)
                    project_vT(i, b + 1)
                    softmax_step()
            attention_output(0)
            project_q(H - 1, 1)
            for cb in range(CB):
                output_projection(0, (cb,))
            project_k(H - 1, 1)
            for mb in range(0, MB, 2):
                softmax_step()
                first_layer(0, (mb, mb + 1))
            early = (0, 1)
            second_layer(early[0], 0)
            attention_output(1)

        with tc.tile_pool(name="store", bufs=1) as store:
            window = [store.tile([P, S], F32, name=f"window{cb}") for cb in range(CB)]
            for cb in range(CB):
                nc.sync.dma_start(window[cb][:], base[rows(cb), :])

            output_projection(1, (0, 1))
            output_projection(1, (2, 3))
            second_layer(early[1], 0)
            for mb in range(0, MB, 2):
                first_layer(1, (mb, mb + 1))

            for cb in range(CB):
                for i in range(HALVES):
                    if i > 0 or cb not in early:
                        second_layer(cb, i)
                nc.vector.tensor_tensor(window[cb][:].indirect(offsets[:]), x1[cb][:], y_sb[cb][:], ALU.add)
                nc.sync.dma_start(out[rows(cb), 0 : S // 2], window[cb][:, 0 : S // 2])
                nc.sync.dma_start(out[rows(cb), S // 2 : S], window[cb][:, S // 2 : S])
